import numpy as np
import ml_dtypes


def mxq(x, axis, fmt="e4m3"):
    dtype, down = {"e4m3": (ml_dtypes.float8_e4m3fn, 7), "e5m2": (ml_dtypes.float8_e5m2, 14)}[fmt]
    v = np.moveaxis(np.asarray(x, np.float32).astype(ml_dtypes.bfloat16).astype(np.float64), axis, -1)
    blocks = v.reshape(v.shape[:-1] + (-1, 32))
    amax = np.abs(blocks).max(-1, keepdims=True)
    byte = np.maximum(np.where(amax > 0, np.frexp(amax)[1] - 1 + 127, 0) - down, 1)
    scale = np.exp2(byte - 127.0)
    codes = (blocks / scale).astype(np.float32).astype(dtype).astype(np.float64)
    return np.moveaxis((codes * scale).reshape(v.shape), -1, axis)


WIDE = False


def mx_kscale(k):
    if not WIDE:
        return np.ones(k)
    levels = np.array([10, -10, 5, -5, 0])
    a = np.random.permutation(np.resize(levels, k // 512 * 4)).reshape(k // 512, 4)
    idx = np.arange(k)
    return np.exp2(a[idx // 512, idx % 128 // 32])


BF16 = ml_dtypes.bfloat16


def bf(x):
    return np.asarray(x, np.float32).astype(BF16)


def f64(x):
    return np.asarray(x).astype(np.float64)


T, B, D, U, V, E = 4, 128, 512, 512, 64, 8
G = 2 * E


def softmax(v):
    e = np.exp(v - v.max(-1, keepdims=True))
    return e / e.sum(-1, keepdims=True)


def setup_inputs():
    rn = np.random.standard_normal
    s = mx_kscale(U)
    return {
        "task_h": bf(np.abs(rn((T, B, U))) * 0.55 * s),
        "share_h": bf(np.abs(rn((B, U))) * 0.5 * s),
        "ews1": bf(rn((U, V, E)) * 2.0 / np.sqrt(U) / s[:, None, None]),
        "ebs1": bf(rn((V, E)) * 0.5),
        "ew1": bf(rn((T, U, V, E)) * 2.0 / np.sqrt(U) / s[None, :, None, None]),
        "eb1": bf(rn((T, V, E)) * 0.5),
        "gate_pre1": bf(rn((T, B, G))),
        "gb1": bf(rn((T, G)) * 0.5),
    }


def reference(task_h, share_h, ews1, ebs1, ew1, eb1, gate_pre1, gb1):
    es = np.maximum((mxq(f64(share_h), 1, "e4m3") @ mxq(f64(ews1).reshape(U, V * E), 0, "e4m3")).reshape(B, V, E) + f64(ebs1), 0.0)
    et = np.maximum((mxq(f64(task_h), 2, "e4m3") @ mxq(f64(ew1).reshape(T, U, V * E), 1, "e4m3")).reshape(T, B, V, E) + f64(eb1)[:, None], 0.0)
    g = softmax(f64(gate_pre1) + f64(gb1)[:, None])
    comb = np.concatenate([et, np.broadcast_to(es, et.shape)], axis=-1)
    return (comb * g[:, :, None, :]).sum(-1)

@@ -1,0 +1,249 @@
+from contextlib import ExitStack
+
+import concourse.mybir as mybir
+from concourse.masks import make_identity
+
+F32 = mybir.dt.float32
+BF16 = mybir.dt.bfloat16
+U32 = mybir.dt.uint32
+U8 = mybir.dt.uint8
+FP8X4 = mybir.dt.float8_e4m3fn_x4
+ALU = mybir.AluOpType
+ACT = mybir.ActivationFunctionType
+AXIS = mybir.AxisListType
+
+T, B, U, V, E = 4, 128, 512, 64, 8
+G = 2 * E
+P = 128
+PACK = 4
+N = V * E
+STREAMS = T + 1
+SHARED = T
+CHUNKS = N // P
+V_CHUNK = P // E
+OWN, COMMON = 0, 1
+VECTOR_COLS = 128
+
+FLOPS = 2 * STREAMS * B * U * N
+
+
+def tile_plelayer_pb_s_kernel(tc, task_h, share_h, ews1, ebs1, ew1, eb1, gate_pre1, gb1, out):
+    nc = tc.nc
+    with ExitStack() as ctx:
+        keep = ctx.enter_context(tc.tile_pool(name="keep", bufs=1))
+        psum_gate = ctx.enter_context(tc.psum_pool(name="psum_gate", bufs=2))
+        psum_work = ctx.enter_context(tc.psum_pool(name="psum_work", bufs=4))
+        psum_out = ctx.enter_context(tc.psum_pool(name="psum_out", bufs=2))
+
+        ident_f32 = keep.tile([P, P], F32)
+        make_identity(nc, ident_f32[:])
+        ident_bf16 = keep.tile([P, P], BF16)
+        make_identity(nc, ident_bf16[:])
+
+        gate_in = keep.tile([P, T, G], BF16)
+        nc.sync.dma_start(out=gate_in[:], in_=gate_pre1.rearrange("t b g -> b t g"))
+        gate_bias = keep.tile([P, T, G], BF16)
+        nc.sync.dma_start(
+            out=gate_bias[:].rearrange("b t g -> b (t g)"),
+            in_=gb1.rearrange("t g -> (t g)").partition_broadcast(P),
+        )
+        bias_rows = keep.tile([P, P], BF16)
+        nc.vector.memset(bias_rows[:], 0.0)
+        nc.sync.dma_start(
+            out=bias_rows[0 : T * CHUNKS, :],
+            in_=eb1.rearrange("t (c v) e -> (t c) (v e)", c=CHUNKS),
+        )
+        nc.sync.dma_start(
+            out=bias_rows[SHARED * CHUNKS : STREAMS * CHUNKS, :],
+            in_=ebs1.rearrange("(c v) e -> c (v e)", c=CHUNKS),
+        )
+
+        w_raw = keep.tile([P, STREAMS, PACK, N], BF16)
+        h_raw = keep.tile([P, STREAMS, U], BF16)
+
+        def load_weights(s):
+            w = ews1 if s == SHARED else ew1[s]
+            nc.sync.dma_start(out=w_raw[:, s], in_=w.rearrange("(p j) v e -> p j (v e)", j=PACK))
+
+        load_weights(SHARED)
+        nc.sync.dma_start(out=h_raw[:, SHARED, :], in_=share_h)
+        load_weights(0)
+        nc.sync.dma_start(out=h_raw[:, 0:T, :], in_=task_h.rearrange("t b u -> b t u"))
+        for s in range(1, T):
+            load_weights(s)
+
+        logits = keep.tile([P, T, G], F32)
+        nc.vector.tensor_tensor(out=logits[:], in0=gate_in[:], in1=gate_bias[:], op=ALU.add)
+        top = keep.tile([P, T], F32)
+        nc.vector.tensor_reduce(out=top[:], in_=logits[:], axis=AXIS.X, op=ALU.max)
+        shifted = keep.tile([P, T, G], F32)
+        nc.vector.tensor_tensor(
+            out=shifted[:],
+            in0=logits[:],
+            in1=top[:].unsqueeze(2).to_broadcast([P, T, G]),
+            op=ALU.subtract,
+        )
+        powers = keep.tile([P, T, G], F32)
+        nc.scalar.activation(out=powers[:], in_=shifted[:], func=ACT.Exp)
+        denom = keep.tile([P, T], F32)
+        nc.vector.tensor_reduce(out=denom[:], in_=powers[:], axis=AXIS.X, op=ALU.add)
+        inv_denom = keep.tile([P, T], F32)
+        nc.vector.reciprocal(out=inv_denom[:], in_=denom[:])
+        gates = keep.tile([P, T, G], F32)
+        nc.vector.tensor_tensor(
+            out=gates[:],
+            in0=powers[:],
+            in1=inv_denom[:].unsqueeze(2).to_broadcast([P, T, G]),
+            op=ALU.mult,
+        )
+        gate_rep = keep.tile([P, 2 * T, V_CHUNK, E], F32)
+        nc.vector.tensor_copy(
+            out=gate_rep[:],
+            in_=gates[:]
+            .rearrange("b t (h e) -> b (t h) e", h=2)
+            .unsqueeze(2)
+            .to_broadcast([P, 2 * T, V_CHUNK, E]),
+        )
+
+        gate_T = []
+        for pair in range(T // 2):
+            bank = psum_gate.tile([P, 4, B], F32, tag="gate", name="gate_T%d" % pair)
+            for i in range(4):
+                nc.tensor.transpose(
+                    bank[:, i, :],
+                    gate_rep[:, 4 * pair + i].rearrange("b v e -> b (v e)"),
+                    ident_f32[:],
+                )
+            gate_T.append(bank)
+
+        bias_ps = psum_work.tile([P, P], BF16, tag="work", name="bias_ps")
+        nc.tensor.transpose(bias_ps[:], bias_rows[:], ident_bf16[:])
+        bias_col = keep.tile([P, STREAMS * CHUNKS], F32)
+        nc.vector.tensor_copy(out=bias_col[:], in_=bias_ps[:, 0 : STREAMS * CHUNKS])
+
+        h_words = (
+            h_raw[:]
+            .rearrange("b s u -> b (s u)")
+            .bitcast(F32)
+            .rearrange("b (s q w) -> b s w q", s=STREAMS, w=2)
+        )
+        h_grouped = keep.tile([P, STREAMS, B * PACK], BF16, align_bytes=64)
+        h_grouped_words = (
+            h_grouped[:]
+            .rearrange("q s x -> q (s x)")
+            .bitcast(F32)
+            .rearrange("q (s b w) -> q s b w", s=STREAMS, w=2)
+        )
+        h_codes = keep.tile([P, STREAMS, B], U32, align_bytes=64)
+        h_scales = keep.tile([P, STREAMS, B], U8, align_bytes=64)
+
+        def transpose_activations(first, count):
+            xt = psum_work.tile([P, count, 2, B], F32, tag="work", name="xt")
+            for i in range(count):
+                for w in range(2):
+                    nc.tensor.transpose(xt[:, i, w, :], h_words[:, first + i, w, :], ident_f32[:])
+            nc.scalar.copy(
+                out=h_grouped_words[:, first : first + count],
+                in_=xt[:].rearrange("q s w b -> q s b w"),
+            )
+
+        def quantise_activations(first, count):
+            streams = slice(first, first + count)
+            nc.vector.quantize_mx(
+                out=h_codes[:, streams, :].rearrange("q s b -> q (s b)").bitcast(FP8X4),
+                scales=h_scales[:, streams, :].rearrange("q s b -> q (s b)"),
+                in_=h_grouped[:, streams, :].rearrange("q s x -> q (s x)"),
+            )
+
+        w_grouped = keep.tile([P, STREAMS, N, PACK], BF16, align_bytes=64)
+        w_codes = keep.tile([P, STREAMS, N], U32, align_bytes=64)
+        w_scales = keep.tile([P, STREAMS, N], U8, align_bytes=64)
+
+        def regroup_weights(s):
+            for copy, cols in (
+                (nc.vector.tensor_copy, slice(0, VECTOR_COLS)),
+                (nc.scalar.copy, slice(VECTOR_COLS, N)),
+            ):
+                copy(
+                    out=w_grouped[:, s, cols, :].rearrange("p (c i) j -> p c j i", i=4),
+                    in_=w_raw[:, s, :, cols].rearrange("p j (c i) -> p c j i", i=4),
+                )
+
+        def quantise_weights(s):
+            nc.vector.quantize_mx(
+                out=w_codes[:, s, :].bitcast(FP8X4),
+                scales=w_scales[:, s, :],
+                in_=w_grouped[:, s].rearrange("p n j -> p (n j)"),
+            )
+
+        def experts(s):
+            acc = psum_work.tile([P, CHUNKS, B], F32, tag="work", name="acc")
+            hidden = keep.tile([P, CHUNKS, B], F32, name="hidden%d" % s)
+            for c in range(CHUNKS):
+                cols = slice(c * P, (c + 1) * P)
+                nc.tensor.matmul_mx(
+                    out=acc[:, c, :],
+                    lhsT=w_codes[:, s, cols].bitcast(FP8X4),
+                    lhsT_scale=w_scales[:, s, cols],
+                    rhs=h_codes[:, s, :].bitcast(FP8X4),
+                    rhs_scale=h_scales[:, s, :],
+                    start=True,
+                    stop=True,
+                )
+            for c in range(CHUNKS):
+                nc.scalar.activation(
+                    out=hidden[:, c, :],
+                    in_=acc[:, c, :],
+                    func=ACT.Relu,
+                    bias=bias_col[:, s * CHUNKS + c : s * CHUNKS + c + 1],
+                )
+            return hidden
+
+        out_sb = keep.tile([P, T, V], F32)
+
+        def gated(hidden, t, half):
+            weighted = keep.tile([P, CHUNKS, B], F32, name="weighted%d_%d" % (t, half))
+            nc.vector.tensor_tensor(
+                out=weighted[:],
+                in0=hidden[:],
+                in1=gate_T[t // 2][:, 2 * (t % 2) + half, :].unsqueeze(1).to_broadcast([P, CHUNKS, B]),
+                op=ALU.mult,
+            )
+            return weighted
+
+        def mix(t, hidden_own, hidden_common):
+            parts = (gated(hidden_common, t, COMMON), gated(hidden_own, t, OWN))
+            total = psum_out.tile([P, CHUNKS, P], F32, tag="total", name="total")
+            for i, weighted in enumerate(parts):
+                for c in range(CHUNKS):
+                    nc.tensor.matmul(
+                        out=total[:, c, :],
+                        lhsT=weighted[:, c, :],
+                        rhs=ident_f32[:],
+                        is_transpose=True,
+                        start=(i == 0 and c == 0),
+                        stop=(i == 1 and c == CHUNKS - 1),
+                    )
+            nc.vector.tensor_reduce(
+                out=out_sb[:, t, :],
+                in_=total[:].rearrange("b c (v e) -> b (c v) e", e=E),
+                axis=AXIS.X,
+                op=ALU.add,
+            )
+            nc.sync.dma_start(out=out[t], in_=out_sb[:, t, :])
+
+        regroup_weights(SHARED)
+        transpose_activations(SHARED, 1)
+        quantise_activations(SHARED, 1)
+        regroup_weights(0)
+        quantise_weights(SHARED)
+        transpose_activations(0, 2)
+        transpose_activations(2, 2)
+        quantise_activations(0, T)
+        hidden_common = experts(SHARED)
+        for t in range(T):
+            if t + 1 < T:
+                regroup_weights(t + 1)
+            quantise_weights(t)
+            hidden_own = experts(t)
+            mix(t, hidden_own, hidden_common)

@@ -22,7 +22,7 @@ SHARED = T
 CHUNKS = N // P
 V_CHUNK = P // E
 OWN, COMMON = 0, 1
-VECTOR_COLS = 128
+VECTOR_COLS = 192
 
 FLOPS = 2 * STREAMS * B * U * N
 
@@ -32,8 +32,9 @@ def tile_plelayer_pb_s_kernel(tc, task_h, share_h, ews1, ebs1, ew1, eb1, gate_pr
     with ExitStack() as ctx:
         keep = ctx.enter_context(tc.tile_pool(name="keep", bufs=1))
         psum_gate = ctx.enter_context(tc.psum_pool(name="psum_gate", bufs=2))
-        psum_work = ctx.enter_context(tc.psum_pool(name="psum_work", bufs=4))
-        psum_out = ctx.enter_context(tc.psum_pool(name="psum_out", bufs=2))
+        psum_work = ctx.enter_context(tc.psum_pool(name="psum_work", bufs=3))
+        psum_total = ctx.enter_context(tc.psum_pool(name="psum_total", bufs=3))
+        ctx.enter_context(tc.manual_schedule())
 
         ident_f32 = keep.tile([P, P], F32)
         make_identity(nc, ident_f32[:])
@@ -41,14 +42,23 @@ def tile_plelayer_pb_s_kernel(tc, task_h, share_h, ews1, ebs1, ew1, eb1, gate_pr
         make_identity(nc, ident_bf16[:])
 
         gate_in = keep.tile([P, T, G], BF16)
-        nc.sync.dma_start(out=gate_in[:], in_=gate_pre1.rearrange("t b g -> b t g"))
         gate_bias = keep.tile([P, T, G], BF16)
+        bias_rows = keep.tile([P, P], BF16)
+        w_raw = keep.tile([P, STREAMS, PACK, N], BF16)
+        h_raw = keep.tile([P, STREAMS, U], BF16)
+
+        def load_weights(s):
+            w = ews1 if s == SHARED else ew1[s]
+            nc.sync.dma_start(out=w_raw[:, s], in_=w.rearrange("(p j) v e -> p j (v e)", j=PACK))
+
+        nc.vector.memset(bias_rows[:], 0.0)
+        nc.sync.dma_start(out=gate_in[:], in_=gate_pre1.rearrange("t b g -> b t g"))
         nc.sync.dma_start(
             out=gate_bias[:].rearrange("b t g -> b (t g)"),
             in_=gb1.rearrange("t g -> (t g)").partition_broadcast(P),
         )
-        bias_rows = keep.tile([P, P], BF16)
-        nc.vector.memset(bias_rows[:], 0.0)
+        load_weights(SHARED)
+        nc.sync.dma_start(out=h_raw[:, SHARED, :], in_=share_h)
         nc.sync.dma_start(
             out=bias_rows[0 : T * CHUNKS, :],
             in_=eb1.rearrange("t (c v) e -> (t c) (v e)", c=CHUNKS),
@@ -57,16 +67,6 @@ def tile_plelayer_pb_s_kernel(tc, task_h, share_h, ews1, ebs1, ew1, eb1, gate_pr
             out=bias_rows[SHARED * CHUNKS : STREAMS * CHUNKS, :],
             in_=ebs1.rearrange("(c v) e -> c (v e)", c=CHUNKS),
         )
-
-        w_raw = keep.tile([P, STREAMS, PACK, N], BF16)
-        h_raw = keep.tile([P, STREAMS, U], BF16)
-
-        def load_weights(s):
-            w = ews1 if s == SHARED else ew1[s]
-            nc.sync.dma_start(out=w_raw[:, s], in_=w.rearrange("(p j) v e -> p j (v e)", j=PACK))
-
-        load_weights(SHARED)
-        nc.sync.dma_start(out=h_raw[:, SHARED, :], in_=share_h)
         load_weights(0)
         nc.sync.dma_start(out=h_raw[:, 0:T, :], in_=task_h.rearrange("t b u -> b t u"))
         for s in range(1, T):
@@ -104,22 +104,6 @@ def tile_plelayer_pb_s_kernel(tc, task_h, share_h, ews1, ebs1, ew1, eb1, gate_pr
             .unsqueeze(2)
             .to_broadcast([P, 2 * T, V_CHUNK, E]),
         )
-
-        gate_T = []
-        for pair in range(T // 2):
-            bank = psum_gate.tile([P, 4, B], F32, tag="gate", name="gate_T%d" % pair)
-            for i in range(4):
-                nc.tensor.transpose(
-                    bank[:, i, :],
-                    gate_rep[:, 4 * pair + i].rearrange("b v e -> b (v e)"),
-                    ident_f32[:],
-                )
-            gate_T.append(bank)
-
-        bias_ps = psum_work.tile([P, P], BF16, tag="work", name="bias_ps")
-        nc.tensor.transpose(bias_ps[:], bias_rows[:], ident_bf16[:])
-        bias_col = keep.tile([P, STREAMS * CHUNKS], F32)
-        nc.vector.tensor_copy(out=bias_col[:], in_=bias_ps[:, 0 : STREAMS * CHUNKS])
 
         h_words = (
             h_raw[:]
@@ -160,14 +144,14 @@ def tile_plelayer_pb_s_kernel(tc, task_h, share_h, ews1, ebs1, ew1, eb1, gate_pr
         w_scales = keep.tile([P, STREAMS, N], U8, align_bytes=64)
 
         def regroup_weights(s):
-            for copy, cols in (
-                (nc.vector.tensor_copy, slice(0, VECTOR_COLS)),
-                (nc.scalar.copy, slice(VECTOR_COLS, N)),
-            ):
-                copy(
-                    out=w_grouped[:, s, cols, :].rearrange("p (c i) j -> p c j i", i=4),
-                    in_=w_raw[:, s, :, cols].rearrange("p j (c i) -> p c j i", i=4),
-                )
+            nc.vector.tensor_copy(
+                out=w_grouped[:, s, 0:VECTOR_COLS, :].rearrange("p (c i) j -> p c j i", i=4),
+                in_=w_raw[:, s, :, 0:VECTOR_COLS].rearrange("p j (c i) -> p c j i", i=4),
+            )
+            nc.scalar.copy(
+                out=w_grouped[:, s, VECTOR_COLS:N, :].rearrange("p (c i) j -> p c j i", i=4),
+                in_=w_raw[:, s, :, VECTOR_COLS:N].rearrange("p j (c i) -> p c j i", i=4),
+            )
 
         def quantise_weights(s):
             nc.vector.quantize_mx(
@@ -175,6 +159,8 @@ def tile_plelayer_pb_s_kernel(tc, task_h, share_h, ews1, ebs1, ew1, eb1, gate_pr
                 scales=w_scales[:, s, :],
                 in_=w_grouped[:, s].rearrange("p n j -> p (n j)"),
             )
+
+        bias_col = keep.tile([P, STREAMS * CHUNKS], F32)
 
         def experts(s):
             acc = psum_work.tile([P, CHUNKS, B], F32, tag="work", name="acc")
@@ -199,9 +185,11 @@ def tile_plelayer_pb_s_kernel(tc, task_h, share_h, ews1, ebs1, ew1, eb1, gate_pr
                 )
             return hidden
 
+        gate_T = []
+        totals = []
         out_sb = keep.tile([P, T, V], F32)
 
-        def gated(hidden, t, half):
+        def add_weighted(hidden, t, half):
             weighted = keep.tile([P, CHUNKS, B], F32, name="weighted%d_%d" % (t, half))
             nc.vector.tensor_tensor(
                 out=weighted[:],
@@ -209,24 +197,22 @@ def tile_plelayer_pb_s_kernel(tc, task_h, share_h, ews1, ebs1, ew1, eb1, gate_pr
                 in1=gate_T[t // 2][:, 2 * (t % 2) + half, :].unsqueeze(1).to_broadcast([P, CHUNKS, B]),
                 op=ALU.mult,
             )
-            return weighted
+            if half == COMMON:
+                totals.append(psum_total.tile([P, CHUNKS, P], F32, tag="total", name="total"))
+            for c in range(CHUNKS):
+                nc.tensor.matmul(
+                    out=totals[t][:, c, :],
+                    lhsT=weighted[:, c, :],
+                    rhs=ident_f32[:],
+                    is_transpose=True,
+                    start=(half == COMMON and c == 0),
+                    stop=(half == OWN and c == CHUNKS - 1),
+                )
 
-        def mix(t, hidden_own, hidden_common):
-            parts = (gated(hidden_common, t, COMMON), gated(hidden_own, t, OWN))
-            total = psum_out.tile([P, CHUNKS, P], F32, tag="total", name="total")
-            for i, weighted in enumerate(parts):
-                for c in range(CHUNKS):
-                    nc.tensor.matmul(
-                        out=total[:, c, :],
-                        lhsT=weighted[:, c, :],
-                        rhs=ident_f32[:],
-                        is_transpose=True,
-                        start=(i == 0 and c == 0),
-                        stop=(i == 1 and c == CHUNKS - 1),
-                    )
+        def finish(t):
             nc.vector.tensor_reduce(
                 out=out_sb[:, t, :],
-                in_=total[:].rearrange("b c (v e) -> b (c v) e", e=E),
+                in_=totals[t][:].rearrange("b c (v e) -> b (c v) e", e=E),
                 axis=AXIS.X,
                 op=ALU.add,
             )
@@ -235,15 +221,36 @@ def tile_plelayer_pb_s_kernel(tc, task_h, share_h, ews1, ebs1, ew1, eb1, gate_pr
         regroup_weights(SHARED)
         transpose_activations(SHARED, 1)
         quantise_activations(SHARED, 1)
+        for pair in range(T // 2):
+            bank = psum_gate.tile([P, 4, B], F32, tag="gate", name="gate_T%d" % pair)
+            for i in range(4):
+                nc.tensor.transpose(
+                    bank[:, i, :],
+                    gate_rep[:, 4 * pair + i].rearrange("b v e -> b (v e)"),
+                    ident_f32[:],
+                )
+            gate_T.append(bank)
         regroup_weights(0)
         quantise_weights(SHARED)
+        bias_ps = psum_work.tile([P, P], BF16, tag="work", name="bias_ps")
+        nc.tensor.transpose(bias_ps[:], bias_rows[:], ident_bf16[:])
+        nc.vector.tensor_copy(out=bias_col[:], in_=bias_ps[:, 0 : STREAMS * CHUNKS])
+        hidden = [None] * STREAMS
+        hidden[SHARED] = experts(SHARED)
         transpose_activations(0, 2)
         transpose_activations(2, 2)
-        quantise_activations(0, T)
-        hidden_common = experts(SHARED)
-        for t in range(T):
+        for t in range(T + 2):
             if t + 1 < T:
                 regroup_weights(t + 1)
-            quantise_weights(t)
-            hidden_own = experts(t)
-            mix(t, hidden_own, hidden_common)
+            if t < T:
+                quantise_weights(t)
+            if t == 0:
+                quantise_activations(0, T)
+            if t < T:
+                hidden[t] = experts(t)
+            if 1 <= t <= T:
+                add_weighted(hidden[t - 1], t - 1, OWN)
+            if t < T:
+                add_weighted(hidden[SHARED], t, COMMON)
+            if t >= 2:
+                finish(t - 2)

@@ -22,7 +22,7 @@ SHARED = T
 CHUNKS = N // P
 V_CHUNK = P // E
 OWN, COMMON = 0, 1
-VECTOR_COLS = 192
+VECTOR_COLS = 256
 
 FLOPS = 2 * STREAMS * B * U * N
 
@@ -34,7 +34,6 @@ def tile_plelayer_pb_s_kernel(tc, task_h, share_h, ews1, ebs1, ew1, eb1, gate_pr
         psum_gate = ctx.enter_context(tc.psum_pool(name="psum_gate", bufs=2))
         psum_work = ctx.enter_context(tc.psum_pool(name="psum_work", bufs=3))
         psum_total = ctx.enter_context(tc.psum_pool(name="psum_total", bufs=3))
-        ctx.enter_context(tc.manual_schedule())
 
         ident_f32 = keep.tile([P, P], F32)
         make_identity(nc, ident_f32[:])

@@ -14,6 +14,7 @@ AXIS = mybir.AxisListType
 
 T, B, U, V, E = 4, 128, 512, 64, 8
 G = 2 * E
+OWN, COMMON = 0, 1
 P = 128
 PACK = 4
 N = V * E
@@ -21,8 +22,8 @@ STREAMS = T + 1
 SHARED = T
 CHUNKS = N // P
 V_CHUNK = P // E
-OWN, COMMON = 0, 1
-VECTOR_COLS = 256
+BANK = 512
+VECTOR_COLS = N // 2
 
 FLOPS = 2 * STREAMS * B * U * N
 
@@ -41,23 +42,25 @@ def tile_plelayer_pb_s_kernel(tc, task_h, share_h, ews1, ebs1, ew1, eb1, gate_pr
         make_identity(nc, ident_bf16[:])
 
         gate_in = keep.tile([P, T, G], BF16)
+        nc.sync.dma_start(out=gate_in[:], in_=gate_pre1.rearrange("t b g -> b t g"))
         gate_bias = keep.tile([P, T, G], BF16)
-        bias_rows = keep.tile([P, P], BF16)
+        nc.sync.dma_start(
+            out=gate_bias[:].rearrange("b t g -> b (t g)"),
+            in_=gb1.rearrange("t g -> (t g)").partition_broadcast(P),
+        )
+
         w_raw = keep.tile([P, STREAMS, PACK, N], BF16)
-        h_raw = keep.tile([P, STREAMS, U], BF16)
 
         def load_weights(s):
             w = ews1 if s == SHARED else ew1[s]
             nc.sync.dma_start(out=w_raw[:, s], in_=w.rearrange("(p j) v e -> p j (v e)", j=PACK))
 
-        nc.vector.memset(bias_rows[:], 0.0)
-        nc.sync.dma_start(out=gate_in[:], in_=gate_pre1.rearrange("t b g -> b t g"))
-        nc.sync.dma_start(
-            out=gate_bias[:].rearrange("b t g -> b (t g)"),
-            in_=gb1.rearrange("t g -> (t g)").partition_broadcast(P),
-        )
+        h_raw = keep.tile([P, STREAMS, U], BF16)
         load_weights(SHARED)
         nc.sync.dma_start(out=h_raw[:, SHARED, :], in_=share_h)
+
+        bias_rows = keep.tile([P, P], BF16)
+        nc.vector.memset(bias_rows[:], 0.0)
         nc.sync.dma_start(
             out=bias_rows[0 : T * CHUNKS, :],
             in_=eb1.rearrange("t (c v) e -> (t c) (v e)", c=CHUNKS),
@@ -66,6 +69,7 @@ def tile_plelayer_pb_s_kernel(tc, task_h, share_h, ews1, ebs1, ew1, eb1, gate_pr
             out=bias_rows[SHARED * CHUNKS : STREAMS * CHUNKS, :],
             in_=ebs1.rearrange("(c v) e -> c (v e)", c=CHUNKS),
         )
+
         load_weights(0)
         nc.sync.dma_start(out=h_raw[:, 0:T, :], in_=task_h.rearrange("t b u -> b t u"))
         for s in range(1, T):
@@ -95,14 +99,35 @@ def tile_plelayer_pb_s_kernel(tc, task_h, share_h, ews1, ebs1, ew1, eb1, gate_pr
             in1=inv_denom[:].unsqueeze(2).to_broadcast([P, T, G]),
             op=ALU.mult,
         )
+
         gate_rep = keep.tile([P, 2 * T, V_CHUNK, E], F32)
         nc.vector.tensor_copy(
             out=gate_rep[:],
             in_=gates[:]
-            .rearrange("b t (h e) -> b (t h) e", h=2)
+            .rearrange("b t (half e) -> b (t half) e", half=2)
             .unsqueeze(2)
             .to_broadcast([P, 2 * T, V_CHUNK, E]),
         )
+        squares = BANK // B
+        gate_banks = []
+        for first in range(0, 2 * T, squares):
+            bank = psum_gate.tile([P, squares, B], F32, tag="gate", name="gate_bank%d" % first)
+            for k in range(squares):
+                nc.tensor.transpose(
+                    bank[:, k, :],
+                    gate_rep[:, first + k].rearrange("b v e -> b (v e)"),
+                    ident_f32[:],
+                )
+            gate_banks.append(bank)
+
+        def gate_T(t, half):
+            square = 2 * t + half
+            return gate_banks[square // squares][:, square % squares, :]
+
+        bias_ps = psum_work.tile([P, P], BF16, tag="work", name="bias_ps")
+        nc.tensor.transpose(bias_ps[:], bias_rows[:], ident_bf16[:])
+        bias_col = keep.tile([P, STREAMS * CHUNKS], F32)
+        nc.vector.tensor_copy(out=bias_col[:], in_=bias_ps[:, 0 : STREAMS * CHUNKS])
 
         h_words = (
             h_raw[:]
@@ -121,13 +146,15 @@ def tile_plelayer_pb_s_kernel(tc, task_h, share_h, ews1, ebs1, ew1, eb1, gate_pr
         h_scales = keep.tile([P, STREAMS, B], U8, align_bytes=64)
 
         def transpose_activations(first, count):
-            xt = psum_work.tile([P, count, 2, B], F32, tag="work", name="xt")
-            for i in range(count):
+            flipped = psum_work.tile([P, count, 2, B], F32, tag="work", name="flipped")
+            for k in range(count):
                 for w in range(2):
-                    nc.tensor.transpose(xt[:, i, w, :], h_words[:, first + i, w, :], ident_f32[:])
+                    nc.tensor.transpose(
+                        flipped[:, k, w, :], h_words[:, first + k, w, :], ident_f32[:]
+                    )
             nc.scalar.copy(
                 out=h_grouped_words[:, first : first + count],
-                in_=xt[:].rearrange("q s w b -> q s b w"),
+                in_=flipped[:].rearrange("q s w b -> q s b w"),
             )
 
         def quantise_activations(first, count):
@@ -138,11 +165,17 @@ def tile_plelayer_pb_s_kernel(tc, task_h, share_h, ews1, ebs1, ew1, eb1, gate_pr
                 in_=h_grouped[:, streams, :].rearrange("q s x -> q (s x)"),
             )
 
+        transpose_activations(SHARED, 1)
+        quantise_activations(SHARED, 1)
+        transpose_activations(0, 2)
+        transpose_activations(2, 2)
+        quantise_activations(0, T)
+
         w_grouped = keep.tile([P, STREAMS, N, PACK], BF16, align_bytes=64)
         w_codes = keep.tile([P, STREAMS, N], U32, align_bytes=64)
         w_scales = keep.tile([P, STREAMS, N], U8, align_bytes=64)
 
-        def regroup_weights(s):
+        def quantise_weights(s):
             nc.vector.tensor_copy(
                 out=w_grouped[:, s, 0:VECTOR_COLS, :].rearrange("p (c i) j -> p c j i", i=4),
                 in_=w_raw[:, s, :, 0:VECTOR_COLS].rearrange("p j (c i) -> p c j i", i=4),
@@ -151,23 +184,19 @@ def tile_plelayer_pb_s_kernel(tc, task_h, share_h, ews1, ebs1, ew1, eb1, gate_pr
                 out=w_grouped[:, s, VECTOR_COLS:N, :].rearrange("p (c i) j -> p c j i", i=4),
                 in_=w_raw[:, s, :, VECTOR_COLS:N].rearrange("p j (c i) -> p c j i", i=4),
             )
-
-        def quantise_weights(s):
             nc.vector.quantize_mx(
                 out=w_codes[:, s, :].bitcast(FP8X4),
                 scales=w_scales[:, s, :],
                 in_=w_grouped[:, s].rearrange("p n j -> p (n j)"),
             )
 
-        bias_col = keep.tile([P, STREAMS * CHUNKS], F32)
-
         def experts(s):
-            acc = psum_work.tile([P, CHUNKS, B], F32, tag="work", name="acc")
-            hidden = keep.tile([P, CHUNKS, B], F32, name="hidden%d" % s)
+            sums = psum_work.tile([P, CHUNKS, B], F32, tag="work", name="sums")
+            expert_out = keep.tile([P, CHUNKS, B], F32, name="expert_out%d" % s)
             for c in range(CHUNKS):
                 cols = slice(c * P, (c + 1) * P)
                 nc.tensor.matmul_mx(
-                    out=acc[:, c, :],
+                    out=sums[:, c, :],
                     lhsT=w_codes[:, s, cols].bitcast(FP8X4),
                     lhsT_scale=w_scales[:, s, cols],
                     rhs=h_codes[:, s, :].bitcast(FP8X4),
@@ -177,79 +206,42 @@ def tile_plelayer_pb_s_kernel(tc, task_h, share_h, ews1, ebs1, ew1, eb1, gate_pr
                 )
             for c in range(CHUNKS):
                 nc.scalar.activation(
-                    out=hidden[:, c, :],
-                    in_=acc[:, c, :],
+                    out=expert_out[:, c, :],
+                    in_=sums[:, c, :],
                     func=ACT.Relu,
                     bias=bias_col[:, s * CHUNKS + c : s * CHUNKS + c + 1],
                 )
-            return hidden
+            return expert_out
 
-        gate_T = []
-        totals = []
+        expert_outs = {}
+        for s in [SHARED] + list(range(T)):
+            quantise_weights(s)
+            expert_outs[s] = experts(s)
+
         out_sb = keep.tile([P, T, V], F32)
-
-        def add_weighted(hidden, t, half):
-            weighted = keep.tile([P, CHUNKS, B], F32, name="weighted%d_%d" % (t, half))
-            nc.vector.tensor_tensor(
-                out=weighted[:],
-                in0=hidden[:],
-                in1=gate_T[t // 2][:, 2 * (t % 2) + half, :].unsqueeze(1).to_broadcast([P, CHUNKS, B]),
-                op=ALU.mult,
-            )
-            if half == COMMON:
-                totals.append(psum_total.tile([P, CHUNKS, P], F32, tag="total", name="total"))
-            for c in range(CHUNKS):
-                nc.tensor.matmul(
-                    out=totals[t][:, c, :],
-                    lhsT=weighted[:, c, :],
-                    rhs=ident_f32[:],
-                    is_transpose=True,
-                    start=(half == COMMON and c == 0),
-                    stop=(half == OWN and c == CHUNKS - 1),
+        for t in range(T):
+            total = psum_total.tile([P, CHUNKS, P], F32, tag="total", name="total")
+            for half, s in ((COMMON, SHARED), (OWN, t)):
+                weighted = keep.tile([P, CHUNKS, B], F32, name="weighted%d_%d" % (t, half))
+                nc.vector.tensor_tensor(
+                    out=weighted[:],
+                    in0=expert_outs[s][:],
+                    in1=gate_T(t, half).unsqueeze(1).to_broadcast([P, CHUNKS, B]),
+                    op=ALU.mult,
                 )
-
-        def finish(t):
+                for c in range(CHUNKS):
+                    nc.tensor.matmul(
+                        out=total[:, c, :],
+                        lhsT=weighted[:, c, :],
+                        rhs=ident_f32[:],
+                        is_transpose=True,
+                        start=(half == COMMON and c == 0),
+                        stop=(half == OWN and c == CHUNKS - 1),
+                    )
             nc.vector.tensor_reduce(
                 out=out_sb[:, t, :],
-                in_=totals[t][:].rearrange("b c (v e) -> b (c v) e", e=E),
+                in_=total[:].rearrange("b c (v e) -> b (c v) e", e=E),
                 axis=AXIS.X,
                 op=ALU.add,
             )
             nc.sync.dma_start(out=out[t], in_=out_sb[:, t, :])
-
-        regroup_weights(SHARED)
-        transpose_activations(SHARED, 1)
-        quantise_activations(SHARED, 1)
-        for pair in range(T // 2):
-            bank = psum_gate.tile([P, 4, B], F32, tag="gate", name="gate_T%d" % pair)
-            for i in range(4):
-                nc.tensor.transpose(
-                    bank[:, i, :],
-                    gate_rep[:, 4 * pair + i].rearrange("b v e -> b (v e)"),
-                    ident_f32[:],
-                )
-            gate_T.append(bank)
-        regroup_weights(0)
-        quantise_weights(SHARED)
-        bias_ps = psum_work.tile([P, P], BF16, tag="work", name="bias_ps")
-        nc.tensor.transpose(bias_ps[:], bias_rows[:], ident_bf16[:])
-        nc.vector.tensor_copy(out=bias_col[:], in_=bias_ps[:, 0 : STREAMS * CHUNKS])
-        hidden = [None] * STREAMS
-        hidden[SHARED] = experts(SHARED)
-        transpose_activations(0, 2)
-        transpose_activations(2, 2)
-        for t in range(T + 2):
-            if t + 1 < T:
-                regroup_weights(t + 1)
-            if t < T:
-                quantise_weights(t)
-            if t == 0:
-                quantise_activations(0, T)
-            if t < T:
-                hidden[t] = experts(t)
-            if 1 <= t <= T:
-                add_weighted(hidden[t - 1], t - 1, OWN)
-            if t < T:
-                add_weighted(hidden[SHARED], t, COMMON)
-            if t >= 2:
-                finish(t - 2)

@@ -33,8 +33,10 @@ def tile_plelayer_pb_s_kernel(tc, task_h, share_h, ews1, ebs1, ew1, eb1, gate_pr
     with ExitStack() as ctx:
         keep = ctx.enter_context(tc.tile_pool(name="keep", bufs=1))
         psum_gate = ctx.enter_context(tc.psum_pool(name="psum_gate", bufs=2))
-        psum_work = ctx.enter_context(tc.psum_pool(name="psum_work", bufs=3))
-        psum_total = ctx.enter_context(tc.psum_pool(name="psum_total", bufs=3))
+        psum_work = ctx.enter_context(tc.psum_pool(name="psum_work", bufs=6))
+        psum_total = psum_work
+
+        ctx.enter_context(tc.manual_schedule())
 
         ident_f32 = keep.tile([P, P], F32)
         make_identity(nc, ident_f32[:])
@@ -55,9 +57,10 @@ def tile_plelayer_pb_s_kernel(tc, task_h, share_h, ews1, ebs1, ew1, eb1, gate_pr
             w = ews1 if s == SHARED else ew1[s]
             nc.sync.dma_start(out=w_raw[:, s], in_=w.rearrange("(p j) v e -> p j (v e)", j=PACK))
 
-        h_raw = keep.tile([P, STREAMS, U], BF16)
+        h_shared = keep.tile([P, U], BF16)
+        h_tasks = keep.tile([P, T, U], BF16)
         load_weights(SHARED)
-        nc.sync.dma_start(out=h_raw[:, SHARED, :], in_=share_h)
+        nc.sync.dma_start(out=h_shared[:], in_=share_h)
 
         bias_rows = keep.tile([P, P], BF16)
         nc.vector.memset(bias_rows[:], 0.0)
@@ -71,70 +74,26 @@ def tile_plelayer_pb_s_kernel(tc, task_h, share_h, ews1, ebs1, ew1, eb1, gate_pr
         )
 
         load_weights(0)
-        nc.sync.dma_start(out=h_raw[:, 0:T, :], in_=task_h.rearrange("t b u -> b t u"))
+        nc.sync.dma_start(out=h_tasks[:], in_=task_h.rearrange("t b u -> b t u"))
         for s in range(1, T):
             load_weights(s)
 
-        logits = keep.tile([P, T, G], F32)
-        nc.vector.tensor_tensor(out=logits[:], in0=gate_in[:], in1=gate_bias[:], op=ALU.add)
-        top = keep.tile([P, T], F32)
-        nc.vector.tensor_reduce(out=top[:], in_=logits[:], axis=AXIS.X, op=ALU.max)
-        shifted = keep.tile([P, T, G], F32)
-        nc.vector.tensor_tensor(
-            out=shifted[:],
-            in0=logits[:],
-            in1=top[:].unsqueeze(2).to_broadcast([P, T, G]),
-            op=ALU.subtract,
-        )
-        powers = keep.tile([P, T, G], F32)
-        nc.scalar.activation(out=powers[:], in_=shifted[:], func=ACT.Exp)
-        denom = keep.tile([P, T], F32)
-        nc.vector.tensor_reduce(out=denom[:], in_=powers[:], axis=AXIS.X, op=ALU.add)
-        inv_denom = keep.tile([P, T], F32)
-        nc.vector.reciprocal(out=inv_denom[:], in_=denom[:])
-        gates = keep.tile([P, T, G], F32)
-        nc.vector.tensor_tensor(
-            out=gates[:],
-            in0=powers[:],
-            in1=inv_denom[:].unsqueeze(2).to_broadcast([P, T, G]),
-            op=ALU.mult,
-        )
-
-        gate_rep = keep.tile([P, 2 * T, V_CHUNK, E], F32)
-        nc.vector.tensor_copy(
-            out=gate_rep[:],
-            in_=gates[:]
-            .rearrange("b t (half e) -> b (t half) e", half=2)
-            .unsqueeze(2)
-            .to_broadcast([P, 2 * T, V_CHUNK, E]),
-        )
-        squares = BANK // B
-        gate_banks = []
-        for first in range(0, 2 * T, squares):
-            bank = psum_gate.tile([P, squares, B], F32, tag="gate", name="gate_bank%d" % first)
-            for k in range(squares):
-                nc.tensor.transpose(
-                    bank[:, k, :],
-                    gate_rep[:, first + k].rearrange("b v e -> b (v e)"),
-                    ident_f32[:],
-                )
-            gate_banks.append(bank)
-
-        def gate_T(t, half):
-            square = 2 * t + half
-            return gate_banks[square // squares][:, square % squares, :]
-
-        bias_ps = psum_work.tile([P, P], BF16, tag="work", name="bias_ps")
-        nc.tensor.transpose(bias_ps[:], bias_rows[:], ident_bf16[:])
         bias_col = keep.tile([P, STREAMS * CHUNKS], F32)
-        nc.vector.tensor_copy(out=bias_col[:], in_=bias_ps[:, 0 : STREAMS * CHUNKS])
 
-        h_words = (
-            h_raw[:]
-            .rearrange("b s u -> b (s u)")
-            .bitcast(F32)
-            .rearrange("b (s q w) -> b s w q", s=STREAMS, w=2)
-        )
+        bias_banks = []
+
+        def transpose_biases():
+            bias_ps = psum_work.tile([P, P], BF16, tag="work", name="bias_ps")
+            nc.tensor.transpose(bias_ps[:], bias_rows[:], ident_bf16[:])
+            bias_banks.append(bias_ps)
+
+        def copy_biases():
+            nc.vector.tensor_copy(out=bias_col[:], in_=bias_banks[0][:, 0 : STREAMS * CHUNKS])
+
+        def h_words(s):
+            rows = h_shared[:] if s == SHARED else h_tasks[:, s, :]
+            return rows.bitcast(F32).rearrange("b (q w) -> b w q", w=2)
+
         h_grouped = keep.tile([P, STREAMS, B * PACK], BF16, align_bytes=64)
         h_grouped_words = (
             h_grouped[:]
@@ -150,7 +109,7 @@ def tile_plelayer_pb_s_kernel(tc, task_h, share_h, ews1, ebs1, ew1, eb1, gate_pr
             for k in range(count):
                 for w in range(2):
                     nc.tensor.transpose(
-                        flipped[:, k, w, :], h_words[:, first + k, w, :], ident_f32[:]
+                        flipped[:, k, w, :], h_words(first + k)[:, w, :], ident_f32[:]
                     )
             nc.scalar.copy(
                 out=h_grouped_words[:, first : first + count],
@@ -165,17 +124,73 @@ def tile_plelayer_pb_s_kernel(tc, task_h, share_h, ews1, ebs1, ew1, eb1, gate_pr
                 in_=h_grouped[:, streams, :].rearrange("q s x -> q (s x)"),
             )
 
-        transpose_activations(SHARED, 1)
-        quantise_activations(SHARED, 1)
-        transpose_activations(0, 2)
-        transpose_activations(2, 2)
-        quantise_activations(0, T)
+        gate_rep = keep.tile([P, 2 * T, V_CHUNK, E], F32)
+
+        powers = keep.tile([P, T, G], F32)
+        denom = keep.tile([P, T], F32)
+        inv_denom = keep.tile([P, T], F32)
+        gates = keep.tile([P, T, G], F32)
+
+        def softmax_powers():
+            logits = keep.tile([P, T, G], F32)
+            nc.vector.tensor_tensor(out=logits[:], in0=gate_in[:], in1=gate_bias[:], op=ALU.add)
+            top = keep.tile([P, T], F32)
+            nc.vector.tensor_reduce(out=top[:], in_=logits[:], axis=AXIS.X, op=ALU.max)
+            shifted = keep.tile([P, T, G], F32)
+            nc.vector.tensor_tensor(
+                out=shifted[:],
+                in0=logits[:],
+                in1=top[:].unsqueeze(2).to_broadcast([P, T, G]),
+                op=ALU.subtract,
+            )
+            nc.scalar.activation(out=powers[:], in_=shifted[:], func=ACT.Exp)
+
+        def softmax_sum():
+            nc.vector.tensor_reduce(out=denom[:], in_=powers[:], axis=AXIS.X, op=ALU.add)
+
+        def softmax_inverse():
+            nc.vector.reciprocal(out=inv_denom[:], in_=denom[:])
+
+        def softmax_divide():
+            nc.vector.tensor_tensor(
+                out=gates[:],
+                in0=powers[:],
+                in1=inv_denom[:].unsqueeze(2).to_broadcast([P, T, G]),
+                op=ALU.mult,
+            )
+
+        def repeat_gates():
+            nc.vector.tensor_copy(
+                out=gate_rep[:],
+                in_=gates[:]
+                .rearrange("b t (half e) -> b (t half) e", half=2)
+                .unsqueeze(2)
+                .to_broadcast([P, 2 * T, V_CHUNK, E]),
+            )
+
+        squares = BANK // B
+        gate_banks = []
+
+        def transpose_gates():
+            for first in range(0, 2 * T, squares):
+                bank = psum_gate.tile([P, squares, B], F32, tag="gate", name="gate_bank%d" % first)
+                for k in range(squares):
+                    nc.tensor.transpose(
+                        bank[:, k, :],
+                        gate_rep[:, first + k].rearrange("b v e -> b (v e)"),
+                        ident_f32[:],
+                    )
+                gate_banks.append(bank)
+
+        def gate_T(t, half):
+            square = 2 * t + half
+            return gate_banks[square // squares][:, square % squares, :]
 
         w_grouped = keep.tile([P, STREAMS, N, PACK], BF16, align_bytes=64)
         w_codes = keep.tile([P, STREAMS, N], U32, align_bytes=64)
         w_scales = keep.tile([P, STREAMS, N], U8, align_bytes=64)
 
-        def quantise_weights(s):
+        def regroup_weights(s):
             nc.vector.tensor_copy(
                 out=w_grouped[:, s, 0:VECTOR_COLS, :].rearrange("p (c i) j -> p c j i", i=4),
                 in_=w_raw[:, s, :, 0:VECTOR_COLS].rearrange("p j (c i) -> p c j i", i=4),
@@ -184,15 +199,20 @@ def tile_plelayer_pb_s_kernel(tc, task_h, share_h, ews1, ebs1, ew1, eb1, gate_pr
                 out=w_grouped[:, s, VECTOR_COLS:N, :].rearrange("p (c i) j -> p c j i", i=4),
                 in_=w_raw[:, s, :, VECTOR_COLS:N].rearrange("p j (c i) -> p c j i", i=4),
             )
+
+        def quantise_weights(s):
             nc.vector.quantize_mx(
                 out=w_codes[:, s, :].bitcast(FP8X4),
                 scales=w_scales[:, s, :],
                 in_=w_grouped[:, s].rearrange("p n j -> p (n j)"),
             )
 
-        def experts(s):
+        expert_sums = {}
+        expert_outs = {}
+
+        def multiply(s):
             sums = psum_work.tile([P, CHUNKS, B], F32, tag="work", name="sums")
-            expert_out = keep.tile([P, CHUNKS, B], F32, name="expert_out%d" % s)
+            expert_sums[s] = sums
             for c in range(CHUNKS):
                 cols = slice(c * P, (c + 1) * P)
                 nc.tensor.matmul_mx(
@@ -204,44 +224,80 @@ def tile_plelayer_pb_s_kernel(tc, task_h, share_h, ews1, ebs1, ew1, eb1, gate_pr
                     start=True,
                     stop=True,
                 )
+
+        def rectify(s):
+            expert_out = keep.tile([P, CHUNKS, B], F32, name="expert_out%d" % s)
             for c in range(CHUNKS):
                 nc.scalar.activation(
                     out=expert_out[:, c, :],
-                    in_=sums[:, c, :],
+                    in_=expert_sums[s][:, c, :],
                     func=ACT.Relu,
                     bias=bias_col[:, s * CHUNKS + c : s * CHUNKS + c + 1],
                 )
-            return expert_out
-
-        expert_outs = {}
-        for s in [SHARED] + list(range(T)):
-            quantise_weights(s)
-            expert_outs[s] = experts(s)
+            expert_outs[s] = expert_out
 
         out_sb = keep.tile([P, T, V], F32)
-        for t in range(T):
-            total = psum_total.tile([P, CHUNKS, P], F32, tag="total", name="total")
-            for half, s in ((COMMON, SHARED), (OWN, t)):
-                weighted = keep.tile([P, CHUNKS, B], F32, name="weighted%d_%d" % (t, half))
-                nc.vector.tensor_tensor(
-                    out=weighted[:],
-                    in0=expert_outs[s][:],
-                    in1=gate_T(t, half).unsqueeze(1).to_broadcast([P, CHUNKS, B]),
-                    op=ALU.mult,
+        totals = {}
+
+        def weigh(t, half):
+            if half == COMMON:
+                totals[t] = psum_total.tile([P, CHUNKS, P], F32, tag="work", name="total")
+            weighted = keep.tile([P, CHUNKS, B], F32, name="weighted%d_%d" % (t, half))
+            nc.vector.tensor_tensor(
+                out=weighted[:],
+                in0=expert_outs[SHARED if half == COMMON else t][:],
+                in1=gate_T(t, half).unsqueeze(1).to_broadcast([P, CHUNKS, B]),
+                op=ALU.mult,
+            )
+            for c in range(CHUNKS):
+                nc.tensor.matmul(
+                    out=totals[t][:, c, :],
+                    lhsT=weighted[:, c, :],
+                    rhs=ident_f32[:],
+                    is_transpose=True,
+                    start=(half == COMMON and c == 0),
+                    stop=(half == OWN and c == CHUNKS - 1),
                 )
-                for c in range(CHUNKS):
-                    nc.tensor.matmul(
-                        out=total[:, c, :],
-                        lhsT=weighted[:, c, :],
-                        rhs=ident_f32[:],
-                        is_transpose=True,
-                        start=(half == COMMON and c == 0),
-                        stop=(half == OWN and c == CHUNKS - 1),
-                    )
+
+        def finish(t):
             nc.vector.tensor_reduce(
                 out=out_sb[:, t, :],
-                in_=total[:].rearrange("b c (v e) -> b (c v) e", e=E),
+                in_=totals[t][:].rearrange("b c (v e) -> b (c v) e", e=E),
                 axis=AXIS.X,
                 op=ALU.add,
             )
             nc.sync.dma_start(out=out[t], in_=out_sb[:, t, :])
+
+        softmax_powers()
+        regroup_weights(SHARED)
+        transpose_activations(SHARED, 1)
+        transpose_biases()
+        softmax_sum()
+        copy_biases()
+        softmax_inverse()
+        quantise_weights(SHARED)
+        softmax_divide()
+        regroup_weights(0)
+        quantise_activations(SHARED, 1)
+        repeat_gates()
+        transpose_activations(0, 2)
+        transpose_activations(2, 2)
+        multiply(SHARED)
+        transpose_gates()
+        quantise_weights(0)
+        regroup_weights(1)
+        regroup_weights(2)
+        quantise_activations(0, T)
+        multiply(0)
+        regroup_weights(3)
+        for t in range(1, T):
+            quantise_weights(t)
+            multiply(t)
+        rectify(SHARED)
+        for t in range(T):
+            rectify(t)
+        for t in range(T):
+            weigh(t, COMMON)
+            weigh(t, OWN)
+        for t in range(T):
+            finish(t)

@@ -24,6 +24,7 @@ CHUNKS = N // P
 V_CHUNK = P // E
 BANK = 512
 VECTOR_COLS = N // 2
+GPSIMD_TASKS = [2, 3]
 
 FLOPS = 2 * STREAMS * B * U * N
 
@@ -186,6 +187,11 @@ def tile_plelayer_pb_s_kernel(tc, task_h, share_h, ews1, ebs1, ew1, eb1, gate_pr
             square = 2 * t + half
             return gate_banks[square // squares][:, square % squares, :]
 
+        gate_sbuf = keep.tile([P, len(GPSIMD_TASKS), B], F32)
+
+        def copy_gates():
+            nc.scalar.copy(out=gate_sbuf[:], in_=gate_banks[1][:, COMMON::2, :])
+
         w_grouped = keep.tile([P, STREAMS, N, PACK], BF16, align_bytes=64)
         w_codes = keep.tile([P, STREAMS, N], U32, align_bytes=64)
         w_scales = keep.tile([P, STREAMS, N], U8, align_bytes=64)
@@ -243,12 +249,20 @@ def tile_plelayer_pb_s_kernel(tc, task_h, share_h, ews1, ebs1, ew1, eb1, gate_pr
             if half == COMMON:
                 totals[t] = psum_total.tile([P, CHUNKS, P], F32, tag="work", name="total")
             weighted = keep.tile([P, CHUNKS, B], F32, name="weighted%d_%d" % (t, half))
-            nc.vector.tensor_tensor(
-                out=weighted[:],
-                in0=expert_outs[SHARED if half == COMMON else t][:],
-                in1=gate_T(t, half).unsqueeze(1).to_broadcast([P, CHUNKS, B]),
-                op=ALU.mult,
-            )
+            if half == COMMON and t in GPSIMD_TASKS:
+                nc.gpsimd.tensor_tensor(
+                    out=weighted[:],
+                    in0=expert_outs[SHARED][:],
+                    in1=gate_sbuf[:, GPSIMD_TASKS.index(t), :].unsqueeze(1).to_broadcast([P, CHUNKS, B]),
+                    op=ALU.mult,
+                )
+            else:
+                nc.vector.tensor_tensor(
+                    out=weighted[:],
+                    in0=expert_outs[SHARED if half == COMMON else t][:],
+                    in1=gate_T(t, half).unsqueeze(1).to_broadcast([P, CHUNKS, B]),
+                    op=ALU.mult,
+                )
             for c in range(CHUNKS):
                 nc.tensor.matmul(
                     out=totals[t][:, c, :],
@@ -294,7 +308,9 @@ def tile_plelayer_pb_s_kernel(tc, task_h, share_h, ews1, ebs1, ew1, eb1, gate_pr
             quantise_weights(t)
             multiply(t)
         rectify(SHARED)
-        for t in range(T):
+        rectify(0)
+        copy_gates()
+        for t in range(1, T):
             rectify(t)
         for t in range(T):
             weigh(t, COMMON)

@@ -21,10 +21,15 @@ N = V * E
 STREAMS = T + 1
 SHARED = T
 CHUNKS = N // P
-V_CHUNK = P // E
+E_RUN = 4
+RUNS = E // E_RUN
+V_CHUNK = P // E_RUN
+BLOCKS = V // V_CHUNK
 BANK = 512
-VECTOR_COLS = N // 2
+VECTOR_UNITS = V // 2
 GPSIMD_TASKS = [2, 3]
+VECTOR_GATES = [0, 1]
+SCALAR_GATES = [2, 3]
 
 FLOPS = 2 * STREAMS * B * U * N
 
@@ -33,8 +38,8 @@ def tile_plelayer_pb_s_kernel(tc, task_h, share_h, ews1, ebs1, ew1, eb1, gate_pr
     nc = tc.nc
     with ExitStack() as ctx:
         keep = ctx.enter_context(tc.tile_pool(name="keep", bufs=1))
-        psum_gate = ctx.enter_context(tc.psum_pool(name="psum_gate", bufs=2))
-        psum_work = ctx.enter_context(tc.psum_pool(name="psum_work", bufs=6))
+        psum_gate = ctx.enter_context(tc.psum_pool(name="psum_gate", bufs=4))
+        psum_work = ctx.enter_context(tc.psum_pool(name="psum_work", bufs=4))
         psum_total = psum_work
 
         ctx.enter_context(tc.manual_schedule())
@@ -43,14 +48,6 @@ def tile_plelayer_pb_s_kernel(tc, task_h, share_h, ews1, ebs1, ew1, eb1, gate_pr
         make_identity(nc, ident_f32[:])
         ident_bf16 = keep.tile([P, P], BF16)
         make_identity(nc, ident_bf16[:])
-
-        gate_in = keep.tile([P, T, G], BF16)
-        nc.sync.dma_start(out=gate_in[:], in_=gate_pre1.rearrange("t b g -> b t g"))
-        gate_bias = keep.tile([P, T, G], BF16)
-        nc.sync.dma_start(
-            out=gate_bias[:].rearrange("b t g -> b (t g)"),
-            in_=gb1.rearrange("t g -> (t g)").partition_broadcast(P),
-        )
 
         w_raw = keep.tile([P, STREAMS, PACK, N], BF16)
 
@@ -61,17 +58,24 @@ def tile_plelayer_pb_s_kernel(tc, task_h, share_h, ews1, ebs1, ew1, eb1, gate_pr
         h_shared = keep.tile([P, U], BF16)
         h_tasks = keep.tile([P, T, U], BF16)
         load_weights(SHARED)
+        gate_in = keep.tile([P, T, G], BF16)
+        nc.sync.dma_start(out=gate_in[:], in_=gate_pre1.rearrange("t b g -> b t g"))
+        gate_bias = keep.tile([P, T, G], BF16)
+        nc.sync.dma_start(
+            out=gate_bias[:].rearrange("b t g -> b (t g)"),
+            in_=gb1.rearrange("t g -> (t g)").partition_broadcast(P),
+        )
         nc.sync.dma_start(out=h_shared[:], in_=share_h)
 
-        bias_rows = keep.tile([P, P], BF16)
-        nc.vector.memset(bias_rows[:], 0.0)
+        bias_in = keep.tile([P, V_CHUNK, RUNS, E_RUN], BF16)
+        nc.vector.memset(bias_in[:].rearrange("q v r i -> q (v r i)"), 0.0)
         nc.sync.dma_start(
-            out=bias_rows[0 : T * CHUNKS, :],
-            in_=eb1.rearrange("t (c v) e -> (t c) (v e)", c=CHUNKS),
+            out=bias_in[0 : T * BLOCKS].rearrange("q v r i -> q (v r i)"),
+            in_=eb1.rearrange("t (k v) e -> (t k) (v e)", k=BLOCKS),
         )
         nc.sync.dma_start(
-            out=bias_rows[SHARED * CHUNKS : STREAMS * CHUNKS, :],
-            in_=ebs1.rearrange("(c v) e -> c (v e)", c=CHUNKS),
+            out=bias_in[SHARED * BLOCKS : STREAMS * BLOCKS].rearrange("q v r i -> q (v r i)"),
+            in_=ebs1.rearrange("(k v) e -> k (v e)", k=BLOCKS),
         )
 
         load_weights(0)
@@ -79,17 +83,24 @@ def tile_plelayer_pb_s_kernel(tc, task_h, share_h, ews1, ebs1, ew1, eb1, gate_pr
         for s in range(1, T):
             load_weights(s)
 
-        bias_col = keep.tile([P, STREAMS * CHUNKS], F32)
+        bias_rows = keep.tile([P, RUNS, V_CHUNK, E_RUN], BF16)
+        bias_col = keep.tile([P, RUNS, STREAMS * BLOCKS], F32)
 
         bias_banks = []
 
+        def sort_biases():
+            nc.scalar.copy(out=bias_rows[:], in_=bias_in[:].rearrange("q v r i -> q r v i"))
+
         def transpose_biases():
-            bias_ps = psum_work.tile([P, P], BF16, tag="work", name="bias_ps")
-            nc.tensor.transpose(bias_ps[:], bias_rows[:], ident_bf16[:])
+            bias_ps = psum_gate.tile([P, RUNS, P], BF16, tag="gate", name="bias_ps")
+            for r in range(RUNS):
+                nc.tensor.transpose(
+                    bias_ps[:, r, :], bias_rows[:, r].rearrange("q v i -> q (v i)"), ident_bf16[:]
+                )
             bias_banks.append(bias_ps)
 
         def copy_biases():
-            nc.vector.tensor_copy(out=bias_col[:], in_=bias_banks[0][:, 0 : STREAMS * CHUNKS])
+            nc.vector.tensor_copy(out=bias_col[:], in_=bias_banks[0][:, :, 0 : STREAMS * BLOCKS])
 
         def h_words(s):
             rows = h_shared[:] if s == SHARED else h_tasks[:, s, :]
@@ -125,12 +136,11 @@ def tile_plelayer_pb_s_kernel(tc, task_h, share_h, ews1, ebs1, ew1, eb1, gate_pr
                 in_=h_grouped[:, streams, :].rearrange("q s x -> q (s x)"),
             )
 
-        gate_rep = keep.tile([P, 2 * T, V_CHUNK, E], F32)
+        gate_rep = keep.tile([P, T, 2 * RUNS, V_CHUNK, E_RUN], F32)
 
         powers = keep.tile([P, T, G], F32)
         denom = keep.tile([P, T], F32)
         inv_denom = keep.tile([P, T], F32)
-        gates = keep.tile([P, T, G], F32)
 
         def softmax_powers():
             logits = keep.tile([P, T, G], F32)
@@ -152,59 +162,69 @@ def tile_plelayer_pb_s_kernel(tc, task_h, share_h, ews1, ebs1, ew1, eb1, gate_pr
         def softmax_inverse():
             nc.vector.reciprocal(out=inv_denom[:], in_=denom[:])
 
-        def softmax_divide():
+        gates = keep.tile([P, len(VECTOR_GATES), G], F32)
+
+        def repeated(rows):
+            return rows.unsqueeze(2).to_broadcast([P, rows.shape[1], V_CHUNK, E_RUN])
+
+        def divide_and_repeat_gates():
+            count = len(VECTOR_GATES)
             nc.vector.tensor_tensor(
                 out=gates[:],
-                in0=powers[:],
-                in1=inv_denom[:].unsqueeze(2).to_broadcast([P, T, G]),
+                in0=powers[:, 0:count, :],
+                in1=inv_denom[:, 0:count].unsqueeze(2).to_broadcast([P, count, G]),
                 op=ALU.mult,
             )
+            for t in SCALAR_GATES:
+                nc.scalar.activation(
+                    out=gate_rep[:, t],
+                    in_=repeated(powers[:, t, :].rearrange("b (h i) -> b h i", i=E_RUN)),
+                    func=ACT.Copy,
+                    scale=inv_denom[:, t : t + 1],
+                )
 
-        def repeat_gates():
+        def repeat_vector_gates():
             nc.vector.tensor_copy(
-                out=gate_rep[:],
-                in_=gates[:]
-                .rearrange("b t (half e) -> b (t half) e", half=2)
-                .unsqueeze(2)
-                .to_broadcast([P, 2 * T, V_CHUNK, E]),
+                out=gate_rep[:, 0 : len(VECTOR_GATES)].rearrange("b t h v i -> b (t h) v i"),
+                in_=repeated(gates[:].rearrange("b t (h i) -> b (t h) i", i=E_RUN)),
             )
 
-        squares = BANK // B
         gate_banks = []
 
         def transpose_gates():
-            for first in range(0, 2 * T, squares):
-                bank = psum_gate.tile([P, squares, B], F32, tag="gate", name="gate_bank%d" % first)
-                for k in range(squares):
+            for t in range(T):
+                bank = psum_gate.tile([P, 2 * RUNS, B], F32, tag="gate", name="gate_bank%d" % t)
+                for h in range(2 * RUNS):
                     nc.tensor.transpose(
-                        bank[:, k, :],
-                        gate_rep[:, first + k].rearrange("b v e -> b (v e)"),
+                        bank[:, h, :],
+                        gate_rep[:, t, h].rearrange("b v i -> b (v i)"),
                         ident_f32[:],
                     )
                 gate_banks.append(bank)
 
-        def gate_T(t, half):
-            square = 2 * t + half
-            return gate_banks[square // squares][:, square % squares, :]
+        def by_chunk(runs):
+            return runs.unsqueeze(2).to_broadcast([P, RUNS, BLOCKS, B])
 
-        gate_sbuf = keep.tile([P, len(GPSIMD_TASKS), B], F32)
+        def gate_T(t, half):
+            return by_chunk(gate_banks[t][:, half * RUNS : (half + 1) * RUNS, :])
+
+        gate_sbuf = keep.tile([P, len(GPSIMD_TASKS), RUNS, B], F32)
 
         def copy_gates():
-            nc.scalar.copy(out=gate_sbuf[:], in_=gate_banks[1][:, COMMON::2, :])
+            for k, t in enumerate(GPSIMD_TASKS):
+                nc.scalar.copy(
+                    out=gate_sbuf[:, k], in_=gate_banks[t][:, COMMON * RUNS : (COMMON + 1) * RUNS, :]
+                )
 
         w_grouped = keep.tile([P, STREAMS, N, PACK], BF16, align_bytes=64)
         w_codes = keep.tile([P, STREAMS, N], U32, align_bytes=64)
         w_scales = keep.tile([P, STREAMS, N], U8, align_bytes=64)
 
         def regroup_weights(s):
-            nc.vector.tensor_copy(
-                out=w_grouped[:, s, 0:VECTOR_COLS, :].rearrange("p (c i) j -> p c j i", i=4),
-                in_=w_raw[:, s, :, 0:VECTOR_COLS].rearrange("p j (c i) -> p c j i", i=4),
-            )
-            nc.scalar.copy(
-                out=w_grouped[:, s, VECTOR_COLS:N, :].rearrange("p (c i) j -> p c j i", i=4),
-                in_=w_raw[:, s, :, VECTOR_COLS:N].rearrange("p j (c i) -> p c j i", i=4),
-            )
+            grouped = w_grouped[:, s].rearrange("p (r v i) j -> p v r j i", r=RUNS, i=E_RUN)
+            raw = w_raw[:, s].rearrange("p j (v r i) -> p v r j i", r=RUNS, i=E_RUN)
+            nc.vector.tensor_copy(out=grouped[:, 0:VECTOR_UNITS], in_=raw[:, 0:VECTOR_UNITS])
+            nc.scalar.copy(out=grouped[:, VECTOR_UNITS:V], in_=raw[:, VECTOR_UNITS:V])
 
         def quantise_weights(s):
             nc.vector.quantize_mx(
@@ -234,38 +254,42 @@ def tile_plelayer_pb_s_kernel(tc, task_h, share_h, ews1, ebs1, ew1, eb1, gate_pr
         def rectify(s):
             expert_out = keep.tile([P, CHUNKS, B], F32, name="expert_out%d" % s)
             for c in range(CHUNKS):
+                column = s * BLOCKS + c % BLOCKS
                 nc.scalar.activation(
                     out=expert_out[:, c, :],
                     in_=expert_sums[s][:, c, :],
                     func=ACT.Relu,
-                    bias=bias_col[:, s * CHUNKS + c : s * CHUNKS + c + 1],
+                    bias=bias_col[:, c // BLOCKS, column : column + 1],
                 )
             expert_outs[s] = expert_out
 
         out_sb = keep.tile([P, T, V], F32)
         totals = {}
 
+        def by_run(chunks):
+            return chunks[:].rearrange("p (r k) b -> p r k b", r=RUNS)
+
         def weigh(t, half):
             if half == COMMON:
-                totals[t] = psum_total.tile([P, CHUNKS, P], F32, tag="work", name="total")
+                totals[t] = psum_total.tile([P, BLOCKS, P], F32, tag="work", name="total")
             weighted = keep.tile([P, CHUNKS, B], F32, name="weighted%d_%d" % (t, half))
             if half == COMMON and t in GPSIMD_TASKS:
                 nc.gpsimd.tensor_tensor(
-                    out=weighted[:],
-                    in0=expert_outs[SHARED][:],
-                    in1=gate_sbuf[:, GPSIMD_TASKS.index(t), :].unsqueeze(1).to_broadcast([P, CHUNKS, B]),
+                    out=by_run(weighted),
+                    in0=by_run(expert_outs[SHARED]),
+                    in1=by_chunk(gate_sbuf[:, GPSIMD_TASKS.index(t)]),
                     op=ALU.mult,
                 )
             else:
                 nc.vector.tensor_tensor(
-                    out=weighted[:],
-                    in0=expert_outs[SHARED if half == COMMON else t][:],
-                    in1=gate_T(t, half).unsqueeze(1).to_broadcast([P, CHUNKS, B]),
+                    out=by_run(weighted),
+                    in0=by_run(expert_outs[SHARED if half == COMMON else t]),
+                    in1=gate_T(t, half),
                     op=ALU.mult,
                 )
             for c in range(CHUNKS):
                 nc.tensor.matmul(
-                    out=totals[t][:, c, :],
+                    out=totals[t][:, c % BLOCKS, :],
                     lhsT=weighted[:, c, :],
                     rhs=ident_f32[:],
                     is_transpose=True,
@@ -276,29 +300,30 @@ def tile_plelayer_pb_s_kernel(tc, task_h, share_h, ews1, ebs1, ew1, eb1, gate_pr
         def finish(t):
             nc.vector.tensor_reduce(
                 out=out_sb[:, t, :],
-                in_=totals[t][:].rearrange("b c (v e) -> b (c v) e", e=E),
+                in_=totals[t][:].rearrange("b k (v i) -> b (k v) i", i=E_RUN),
                 axis=AXIS.X,
                 op=ALU.add,
             )
             nc.sync.dma_start(out=out[t], in_=out_sb[:, t, :])
 
-        softmax_powers()
         regroup_weights(SHARED)
+        sort_biases()
+        softmax_powers()
         transpose_activations(SHARED, 1)
         transpose_biases()
         softmax_sum()
         copy_biases()
         softmax_inverse()
         quantise_weights(SHARED)
-        softmax_divide()
         regroup_weights(0)
+        divide_and_repeat_gates()
         quantise_activations(SHARED, 1)
-        repeat_gates()
+        quantise_weights(0)
+        repeat_vector_gates()
         transpose_activations(0, 2)
         transpose_activations(2, 2)
         multiply(SHARED)
         transpose_gates()
-        quantise_weights(0)
         regroup_weights(1)
         regroup_weights(2)
         quantise_activations(0, T)

@@ -236,9 +236,22 @@ def tile_plelayer_pb_s_kernel(tc, task_h, share_h, ews1, ebs1, ew1, eb1, gate_pr
         expert_sums = {}
         expert_outs = {}
 
-        def multiply(s):
+        def keep_busy(s, passes):
             sums = psum_work.tile([P, CHUNKS, B], F32, tag="work", name="sums")
             expert_sums[s] = sums
+            for k in range(passes):
+                nc.tensor.matmul_mx(
+                    out=sums[:].rearrange("p c b -> p (c b)"),
+                    lhsT=h_codes[:, SHARED, :].bitcast(FP8X4),
+                    lhsT_scale=h_scales[:, SHARED, :],
+                    rhs=w_codes[:, SHARED, :].bitcast(FP8X4),
+                    rhs_scale=w_scales[:, SHARED, :],
+                    start=True,
+                    stop=True,
+                )
+
+        def multiply(s):
+            sums = expert_sums[s]
             for c in range(CHUNKS):
                 cols = slice(c * P, (c + 1) * P)
                 nc.tensor.matmul_mx(
@@ -322,7 +335,9 @@ def tile_plelayer_pb_s_kernel(tc, task_h, share_h, ews1, ebs1, ew1, eb1, gate_pr
         repeat_vector_gates()
         transpose_activations(0, 2)
         transpose_activations(2, 2)
+        keep_busy(SHARED, 0)
         multiply(SHARED)
+        keep_busy(0, 3)
         transpose_gates()
         regroup_weights(1)
         regroup_weights(2)
@@ -331,6 +346,7 @@ def tile_plelayer_pb_s_kernel(tc, task_h, share_h, ews1, ebs1, ew1, eb1, gate_pr
         regroup_weights(3)
         for t in range(1, T):
             quantise_weights(t)
+            keep_busy(t, 2)
             multiply(t)
         rectify(SHARED)
         rectify(0)

@@ -26,7 +26,7 @@ RUNS = E // E_RUN
 V_CHUNK = P // E_RUN
 BLOCKS = V // V_CHUNK
 BANK = 512
-VECTOR_UNITS = V // 2
+VECTOR_UNITS = 36
 GPSIMD_TASKS = [2, 3]
 VECTOR_GATES = [0, 1]
 SCALAR_GATES = [2, 3]
@@ -210,11 +210,11 @@ def tile_plelayer_pb_s_kernel(tc, task_h, share_h, ews1, ebs1, ew1, eb1, gate_pr
 
         gate_sbuf = keep.tile([P, len(GPSIMD_TASKS), RUNS, B], F32)
 
-        def copy_gates():
-            for k, t in enumerate(GPSIMD_TASKS):
-                nc.scalar.copy(
-                    out=gate_sbuf[:, k], in_=gate_banks[t][:, COMMON * RUNS : (COMMON + 1) * RUNS, :]
-                )
+        def copy_gates(t):
+            nc.scalar.copy(
+                out=gate_sbuf[:, GPSIMD_TASKS.index(t)],
+                in_=gate_banks[t][:, COMMON * RUNS : (COMMON + 1) * RUNS, :],
+            )
 
         w_grouped = keep.tile([P, STREAMS, N, PACK], BF16, align_bytes=64)
         w_codes = keep.tile([P, STREAMS, N], U32, align_bytes=64)
@@ -348,13 +348,18 @@ def tile_plelayer_pb_s_kernel(tc, task_h, share_h, ews1, ebs1, ew1, eb1, gate_pr
             quantise_weights(t)
             keep_busy(t, 2)
             multiply(t)
+        copy_gates(2)
         rectify(SHARED)
-        rectify(0)
-        copy_gates()
-        for t in range(1, T):
-            rectify(t)
+        copy_gates(3)
         for t in range(T):
-            weigh(t, COMMON)
-            weigh(t, OWN)
+            rectify(t)
+        weigh(0, COMMON)
+        weigh(1, COMMON)
+        weigh(0, OWN)
+        weigh(1, OWN)
+        weigh(2, COMMON)
+        weigh(2, OWN)
+        weigh(3, COMMON)
+        weigh(3, OWN)
         for t in range(T):
             finish(t)

@@ -26,7 +26,7 @@ RUNS = E // E_RUN
 V_CHUNK = P // E_RUN
 BLOCKS = V // V_CHUNK
 BANK = 512
-VECTOR_UNITS = 36
+VECTOR_UNITS = 38
 GPSIMD_TASKS = [2, 3]
 VECTOR_GATES = [0, 1]
 SCALAR_GATES = [2, 3]
@@ -324,10 +324,10 @@ def tile_plelayer_pb_s_kernel(tc, task_h, share_h, ews1, ebs1, ew1, eb1, gate_pr
         softmax_powers()
         transpose_activations(SHARED, 1)
         transpose_biases()
+        quantise_weights(SHARED)
         softmax_sum()
         copy_biases()
         softmax_inverse()
-        quantise_weights(SHARED)
         regroup_weights(0)
         divide_and_repeat_gates()
         quantise_activations(SHARED, 1)

@@ -49,6 +49,11 @@ def tile_plelayer_pb_s_kernel(tc, task_h, share_h, ews1, ebs1, ew1, eb1, gate_pr
         ident_bf16 = keep.tile([P, P], BF16)
         make_identity(nc, ident_bf16[:])
 
+        gate_bias = keep.tile([P, T * G], BF16)
+        nc.vector.memset(gate_bias[:], 0.0)
+        ones = keep.tile([P, P], BF16)
+        nc.vector.memset(ones[:], 1.0)
+
         w_raw = keep.tile([P, STREAMS, PACK, N], BF16)
 
         def load_weights(s):
@@ -60,10 +65,8 @@ def tile_plelayer_pb_s_kernel(tc, task_h, share_h, ews1, ebs1, ew1, eb1, gate_pr
         load_weights(SHARED)
         gate_in = keep.tile([P, T, G], BF16)
         nc.sync.dma_start(out=gate_in[:], in_=gate_pre1.rearrange("t b g -> b t g"))
-        gate_bias = keep.tile([P, T, G], BF16)
         nc.sync.dma_start(
-            out=gate_bias[:].rearrange("b t g -> b (t g)"),
-            in_=gb1.rearrange("t g -> (t g)").partition_broadcast(P),
+            out=gate_bias[0:1, :], in_=gb1.rearrange("t g -> (t g)").unsqueeze(0)
         )
         nc.sync.dma_start(out=h_shared[:], in_=share_h)
 
@@ -100,7 +103,7 @@ def tile_plelayer_pb_s_kernel(tc, task_h, share_h, ews1, ebs1, ew1, eb1, gate_pr
             bias_banks.append(bias_ps)
 
         def copy_biases():
-            nc.vector.tensor_copy(out=bias_col[:], in_=bias_banks[0][:, :, 0 : STREAMS * BLOCKS])
+            nc.scalar.copy(out=bias_col[:], in_=bias_banks[0][:, :, 0 : STREAMS * BLOCKS])
 
         def h_words(s):
             rows = h_shared[:] if s == SHARED else h_tasks[:, s, :]
@@ -143,8 +146,16 @@ def tile_plelayer_pb_s_kernel(tc, task_h, share_h, ews1, ebs1, ew1, eb1, gate_pr
         inv_denom = keep.tile([P, T], F32)
 
         def softmax_powers():
-            logits = keep.tile([P, T, G], F32)
-            nc.vector.tensor_tensor(out=logits[:], in0=gate_in[:], in1=gate_bias[:], op=ALU.add)
+            logits = psum_work.tile([P, T, G], F32, tag="work", name="logits")
+            flat = logits[:].rearrange("b t g -> b (t g)")
+            nc.tensor.matmul(
+                out=flat,
+                lhsT=ident_bf16[:],
+                rhs=gate_in[:].rearrange("b t g -> b (t g)"),
+                start=True,
+                stop=False,
+            )
+            nc.tensor.matmul(out=flat, lhsT=ones[:], rhs=gate_bias[:], start=False, stop=True)
             top = keep.tile([P, T], F32)
             nc.vector.tensor_reduce(out=top[:], in_=logits[:], axis=AXIS.X, op=ALU.max)
             shifted = keep.tile([P, T, G], F32)
@@ -326,9 +337,9 @@ def tile_plelayer_pb_s_kernel(tc, task_h, share_h, ews1, ebs1, ew1, eb1, gate_pr
         transpose_biases()
         quantise_weights(SHARED)
         softmax_sum()
-        copy_biases()
         softmax_inverse()
         regroup_weights(0)
+        copy_biases()
         divide_and_repeat_gates()
         quantise_activations(SHARED, 1)
         quantise_weights(0)
@@ -356,8 +367,8 @@ def tile_plelayer_pb_s_kernel(tc, task_h, share_h, ews1, ebs1, ew1, eb1, gate_pr
         weigh(0, COMMON)
         weigh(1, COMMON)
         weigh(0, OWN)
-        weigh(1, OWN)
         weigh(2, COMMON)
+        weigh(1, OWN)
         weigh(2, OWN)
         weigh(3, COMMON)
         weigh(3, OWN)

@@ -26,10 +26,8 @@ RUNS = E // E_RUN
 V_CHUNK = P // E_RUN
 BLOCKS = V // V_CHUNK
 BANK = 512
-VECTOR_UNITS = 38
+VECTOR_UNITS = 40
 GPSIMD_TASKS = [2, 3]
-VECTOR_GATES = [0, 1]
-SCALAR_GATES = [2, 3]
 
 FLOPS = 2 * STREAMS * B * U * N
 
@@ -173,31 +171,25 @@ def tile_plelayer_pb_s_kernel(tc, task_h, share_h, ews1, ebs1, ew1, eb1, gate_pr
         def softmax_inverse():
             nc.vector.reciprocal(out=inv_denom[:], in_=denom[:])
 
-        gates = keep.tile([P, len(VECTOR_GATES), G], F32)
+        def repeated(t):
+            runs = powers[:, t, :].rearrange("b (h i) -> b h i", i=E_RUN)
+            return runs.unsqueeze(2).to_broadcast([P, 2 * RUNS, V_CHUNK, E_RUN])
 
-        def repeated(rows):
-            return rows.unsqueeze(2).to_broadcast([P, rows.shape[1], V_CHUNK, E_RUN])
-
-        def divide_and_repeat_gates():
-            count = len(VECTOR_GATES)
-            nc.vector.tensor_tensor(
-                out=gates[:],
-                in0=powers[:, 0:count, :],
-                in1=inv_denom[:, 0:count].unsqueeze(2).to_broadcast([P, count, G]),
-                op=ALU.mult,
+        def gates_by_vector(t):
+            nc.vector.tensor_scalar(
+                out=gate_rep[:, t],
+                in0=repeated(t),
+                scalar1=inv_denom[:, t : t + 1],
+                scalar2=None,
+                op0=ALU.mult,
             )
-            for t in SCALAR_GATES:
-                nc.scalar.activation(
-                    out=gate_rep[:, t],
-                    in_=repeated(powers[:, t, :].rearrange("b (h i) -> b h i", i=E_RUN)),
-                    func=ACT.Copy,
-                    scale=inv_denom[:, t : t + 1],
-                )
 
-        def repeat_vector_gates():
-            nc.vector.tensor_copy(
-                out=gate_rep[:, 0 : len(VECTOR_GATES)].rearrange("b t h v i -> b (t h) v i"),
-                in_=repeated(gates[:].rearrange("b t (h i) -> b (t h) i", i=E_RUN)),
+        def gates_by_scalar(t):
+            nc.scalar.activation(
+                out=gate_rep[:, t],
+                in_=repeated(t),
+                func=ACT.Copy,
+                scale=inv_denom[:, t : t + 1],
             )
 
         gate_banks = []
@@ -340,10 +332,12 @@ def tile_plelayer_pb_s_kernel(tc, task_h, share_h, ews1, ebs1, ew1, eb1, gate_pr
         softmax_inverse()
         regroup_weights(0)
         copy_biases()
-        divide_and_repeat_gates()
+        gates_by_scalar(2)
+        gates_by_scalar(3)
         quantise_activations(SHARED, 1)
         quantise_weights(0)
-        repeat_vector_gates()
+        gates_by_vector(0)
+        gates_by_vector(1)
         transpose_activations(0, 2)
         transpose_activations(2, 2)
         keep_busy(SHARED, 0)

@@ -239,22 +239,9 @@ def tile_plelayer_pb_s_kernel(tc, task_h, share_h, ews1, ebs1, ew1, eb1, gate_pr
         expert_sums = {}
         expert_outs = {}
 
-        def keep_busy(s, passes):
+        def multiply(s):
             sums = psum_work.tile([P, CHUNKS, B], F32, tag="work", name="sums")
             expert_sums[s] = sums
-            for k in range(passes):
-                nc.tensor.matmul_mx(
-                    out=sums[:].rearrange("p c b -> p (c b)"),
-                    lhsT=h_codes[:, SHARED, :].bitcast(FP8X4),
-                    lhsT_scale=h_scales[:, SHARED, :],
-                    rhs=w_codes[:, SHARED, :].bitcast(FP8X4),
-                    rhs_scale=w_scales[:, SHARED, :],
-                    start=True,
-                    stop=True,
-                )
-
-        def multiply(s):
-            sums = expert_sums[s]
             for c in range(CHUNKS):
                 cols = slice(c * P, (c + 1) * P)
                 nc.tensor.matmul_mx(
@@ -340,9 +327,7 @@ def tile_plelayer_pb_s_kernel(tc, task_h, share_h, ews1, ebs1, ew1, eb1, gate_pr
         gates_by_vector(1)
         transpose_activations(0, 2)
         transpose_activations(2, 2)
-        keep_busy(SHARED, 0)
         multiply(SHARED)
-        keep_busy(0, 3)
         transpose_gates()
         regroup_weights(1)
         regroup_weights(2)
@@ -351,7 +336,6 @@ def tile_plelayer_pb_s_kernel(tc, task_h, share_h, ews1, ebs1, ew1, eb1, gate_pr
         regroup_weights(3)
         for t in range(1, T):
             quantise_weights(t)
-            keep_busy(t, 2)
             multiply(t)
         copy_gates(2)
         rectify(SHARED)

@@ -326,19 +326,21 @@ def tile_plelayer_pb_s_kernel(tc, task_h, share_h, ews1, ebs1, ew1, eb1, gate_pr
         gates_by_vector(0)
         gates_by_vector(1)
         transpose_activations(0, 2)
+        regroup_weights(1)
         transpose_activations(2, 2)
         multiply(SHARED)
         transpose_gates()
-        regroup_weights(1)
         regroup_weights(2)
+        quantise_weights(1)
         quantise_activations(0, T)
         multiply(0)
+        multiply(1)
         regroup_weights(3)
-        for t in range(1, T):
+        for t in range(2, T):
             quantise_weights(t)
             multiply(t)
-        copy_gates(2)
         rectify(SHARED)
+        copy_gates(2)
         copy_gates(3)
         for t in range(T):
             rectify(t)

from contextlib import ExitStack

import concourse.mybir as mybir
from concourse.masks import make_identity

F32 = mybir.dt.float32
BF16 = mybir.dt.bfloat16
U32 = mybir.dt.uint32
U8 = mybir.dt.uint8
FP8X4 = mybir.dt.float8_e4m3fn_x4
ALU = mybir.AluOpType
ACT = mybir.ActivationFunctionType
AXIS = mybir.AxisListType

T, B, U, V, E = 4, 128, 512, 64, 8
G = 2 * E
OWN, COMMON = 0, 1
P = 128
PACK = 4
N = V * E
STREAMS = T + 1
SHARED = T
CHUNKS = N // P
E_RUN = 4
RUNS = E // E_RUN
V_CHUNK = P // E_RUN
BLOCKS = V // V_CHUNK
BANK = 512
VECTOR_UNITS = 40
GPSIMD_TASKS = [2, 3]

FLOPS = 2 * STREAMS * B * U * N


def tile_plelayer_pb_s_kernel(tc, task_h, share_h, ews1, ebs1, ew1, eb1, gate_pre1, gb1, out):
    nc = tc.nc
    with ExitStack() as ctx:
        keep = ctx.enter_context(tc.tile_pool(name="keep", bufs=1))
        psum_gate = ctx.enter_context(tc.psum_pool(name="psum_gate", bufs=4))
        psum_work = ctx.enter_context(tc.psum_pool(name="psum_work", bufs=4))
        psum_total = psum_work

        ctx.enter_context(tc.manual_schedule())

        ident_f32 = keep.tile([P, P], F32)
        make_identity(nc, ident_f32[:])
        ident_bf16 = keep.tile([P, P], BF16)
        make_identity(nc, ident_bf16[:])

        gate_bias = keep.tile([P, T * G], BF16)
        nc.vector.memset(gate_bias[:], 0.0)
        ones = keep.tile([P, P], BF16)
        nc.vector.memset(ones[:], 1.0)

        w_raw = keep.tile([P, STREAMS, PACK, N], BF16)

        def load_weights(s):
            w = ews1 if s == SHARED else ew1[s]
            nc.sync.dma_start(out=w_raw[:, s], in_=w.rearrange("(p j) v e -> p j (v e)", j=PACK))

        h_shared = keep.tile([P, U], BF16)
        h_tasks = keep.tile([P, T, U], BF16)
        load_weights(SHARED)
        gate_in = keep.tile([P, T, G], BF16)
        nc.sync.dma_start(out=gate_in[:], in_=gate_pre1.rearrange("t b g -> b t g"))
        nc.sync.dma_start(
            out=gate_bias[0:1, :], in_=gb1.rearrange("t g -> (t g)").unsqueeze(0)
        )
        nc.sync.dma_start(out=h_shared[:], in_=share_h)

        bias_in = keep.tile([P, V_CHUNK, RUNS, E_RUN], BF16)
        nc.vector.memset(bias_in[:].rearrange("q v r i -> q (v r i)"), 0.0)
        nc.sync.dma_start(
            out=bias_in[0 : T * BLOCKS].rearrange("q v r i -> q (v r i)"),
            in_=eb1.rearrange("t (k v) e -> (t k) (v e)", k=BLOCKS),
        )
        nc.sync.dma_start(
            out=bias_in[SHARED * BLOCKS : STREAMS * BLOCKS].rearrange("q v r i -> q (v r i)"),
            in_=ebs1.rearrange("(k v) e -> k (v e)", k=BLOCKS),
        )

        load_weights(0)
        nc.sync.dma_start(out=h_tasks[:], in_=task_h.rearrange("t b u -> b t u"))
        for s in range(1, T):
            load_weights(s)

        bias_rows = keep.tile([P, RUNS, V_CHUNK, E_RUN], BF16)
        bias_col = keep.tile([P, RUNS, STREAMS * BLOCKS], F32)

        bias_banks = []

        def sort_biases():
            nc.scalar.copy(out=bias_rows[:], in_=bias_in[:].rearrange("q v r i -> q r v i"))

        def transpose_biases():
            bias_ps = psum_gate.tile([P, RUNS, P], BF16, tag="gate", name="bias_ps")
            for r in range(RUNS):
                nc.tensor.transpose(
                    bias_ps[:, r, :], bias_rows[:, r].rearrange("q v i -> q (v i)"), ident_bf16[:]
                )
            bias_banks.append(bias_ps)

        def copy_biases():
            nc.scalar.copy(out=bias_col[:], in_=bias_banks[0][:, :, 0 : STREAMS * BLOCKS])

        def h_words(s):
            rows = h_shared[:] if s == SHARED else h_tasks[:, s, :]
            return rows.bitcast(F32).rearrange("b (q w) -> b w q", w=2)

        h_grouped = keep.tile([P, STREAMS, B * PACK], BF16, align_bytes=64)
        h_grouped_words = (
            h_grouped[:]
            .rearrange("q s x -> q (s x)")
            .bitcast(F32)
            .rearrange("q (s b w) -> q s b w", s=STREAMS, w=2)
        )
        h_codes = keep.tile([P, STREAMS, B], U32, align_bytes=64)
        h_scales = keep.tile([P, STREAMS, B], U8, align_bytes=64)

        def transpose_activations(first, count):
            flipped = psum_work.tile([P, count, 2, B], F32, tag="work", name="flipped")
            for k in range(count):
                for w in range(2):
                    nc.tensor.transpose(
                        flipped[:, k, w, :], h_words(first + k)[:, w, :], ident_f32[:]
                    )
            nc.scalar.copy(
                out=h_grouped_words[:, first : first + count],
                in_=flipped[:].rearrange("q s w b -> q s b w"),
            )

        def quantise_activations(first, count):
            streams = slice(first, first + count)
            nc.vector.quantize_mx(
                out=h_codes[:, streams, :].rearrange("q s b -> q (s b)").bitcast(FP8X4),
                scales=h_scales[:, streams, :].rearrange("q s b -> q (s b)"),
                in_=h_grouped[:, streams, :].rearrange("q s x -> q (s x)"),
            )

        gate_rep = keep.tile([P, T, 2 * RUNS, V_CHUNK, E_RUN], F32)

        powers = keep.tile([P, T, G], F32)
        denom = keep.tile([P, T], F32)
        inv_denom = keep.tile([P, T], F32)

        def softmax_powers():
            logits = psum_work.tile([P, T, G], F32, tag="work", name="logits")
            flat = logits[:].rearrange("b t g -> b (t g)")
            nc.tensor.matmul(
                out=flat,
                lhsT=ident_bf16[:],
                rhs=gate_in[:].rearrange("b t g -> b (t g)"),
                start=True,
                stop=False,
            )
            nc.tensor.matmul(out=flat, lhsT=ones[:], rhs=gate_bias[:], start=False, stop=True)
            top = keep.tile([P, T], F32)
            nc.vector.tensor_reduce(out=top[:], in_=logits[:], axis=AXIS.X, op=ALU.max)
            shifted = keep.tile([P, T, G], F32)
            nc.vector.tensor_tensor(
                out=shifted[:],
                in0=logits[:],
                in1=top[:].unsqueeze(2).to_broadcast([P, T, G]),
                op=ALU.subtract,
            )
            nc.scalar.activation(out=powers[:], in_=shifted[:], func=ACT.Exp)

        def softmax_sum():
            nc.vector.tensor_reduce(out=denom[:], in_=powers[:], axis=AXIS.X, op=ALU.add)

        def softmax_inverse():
            nc.vector.reciprocal(out=inv_denom[:], in_=denom[:])

        def repeated(t):
            runs = powers[:, t, :].rearrange("b (h i) -> b h i", i=E_RUN)
            return runs.unsqueeze(2).to_broadcast([P, 2 * RUNS, V_CHUNK, E_RUN])

        def gates_by_vector(t):
            nc.vector.tensor_scalar(
                out=gate_rep[:, t],
                in0=repeated(t),
                scalar1=inv_denom[:, t : t + 1],
                scalar2=None,
                op0=ALU.mult,
            )

        def gates_by_scalar(t):
            nc.scalar.activation(
                out=gate_rep[:, t],
                in_=repeated(t),
                func=ACT.Copy,
                scale=inv_denom[:, t : t + 1],
            )

        gate_banks = []

        def transpose_gates():
            for t in range(T):
                bank = psum_gate.tile([P, 2 * RUNS, B], F32, tag="gate", name="gate_bank%d" % t)
                for h in range(2 * RUNS):
                    nc.tensor.transpose(
                        bank[:, h, :],
                        gate_rep[:, t, h].rearrange("b v i -> b (v i)"),
                        ident_f32[:],
                    )
                gate_banks.append(bank)

        def by_chunk(runs):
            return runs.unsqueeze(2).to_broadcast([P, RUNS, BLOCKS, B])

        def gate_T(t, half):
            return by_chunk(gate_banks[t][:, half * RUNS : (half + 1) * RUNS, :])

        gate_sbuf = keep.tile([P, len(GPSIMD_TASKS), RUNS, B], F32)

        def copy_gates(t):
            nc.scalar.copy(
                out=gate_sbuf[:, GPSIMD_TASKS.index(t)],
                in_=gate_banks[t][:, COMMON * RUNS : (COMMON + 1) * RUNS, :],
            )

        w_grouped = keep.tile([P, STREAMS, N, PACK], BF16, align_bytes=64)
        w_codes = keep.tile([P, STREAMS, N], U32, align_bytes=64)
        w_scales = keep.tile([P, STREAMS, N], U8, align_bytes=64)

        def regroup_weights(s):
            grouped = w_grouped[:, s].rearrange("p (r v i) j -> p v r j i", r=RUNS, i=E_RUN)
            raw = w_raw[:, s].rearrange("p j (v r i) -> p v r j i", r=RUNS, i=E_RUN)
            nc.vector.tensor_copy(out=grouped[:, 0:VECTOR_UNITS], in_=raw[:, 0:VECTOR_UNITS])
            nc.scalar.copy(out=grouped[:, VECTOR_UNITS:V], in_=raw[:, VECTOR_UNITS:V])

        def quantise_weights(s):
            nc.vector.quantize_mx(
                out=w_codes[:, s, :].bitcast(FP8X4),
                scales=w_scales[:, s, :],
                in_=w_grouped[:, s].rearrange("p n j -> p (n j)"),
            )

        expert_sums = {}
        expert_outs = {}

        def multiply(s):
            sums = psum_work.tile([P, CHUNKS, B], F32, tag="work", name="sums")
            expert_sums[s] = sums
            for c in range(CHUNKS):
                cols = slice(c * P, (c + 1) * P)
                nc.tensor.matmul_mx(
                    out=sums[:, c, :],
                    lhsT=w_codes[:, s, cols].bitcast(FP8X4),
                    lhsT_scale=w_scales[:, s, cols],
                    rhs=h_codes[:, s, :].bitcast(FP8X4),
                    rhs_scale=h_scales[:, s, :],
                    start=True,
                    stop=True,
                )

        def rectify(s):
            expert_out = keep.tile([P, CHUNKS, B], F32, name="expert_out%d" % s)
            for c in range(CHUNKS):
                column = s * BLOCKS + c % BLOCKS
                nc.scalar.activation(
                    out=expert_out[:, c, :],
                    in_=expert_sums[s][:, c, :],
                    func=ACT.Relu,
                    bias=bias_col[:, c // BLOCKS, column : column + 1],
                )
            expert_outs[s] = expert_out

        out_sb = keep.tile([P, T, V], F32)
        totals = {}

        def by_run(chunks):
            return chunks[:].rearrange("p (r k) b -> p r k b", r=RUNS)

        def weigh(t, half):
            if half == COMMON:
                totals[t] = psum_total.tile([P, BLOCKS, P], F32, tag="work", name="total")
            weighted = keep.tile([P, CHUNKS, B], F32, name="weighted%d_%d" % (t, half))
            if half == COMMON and t in GPSIMD_TASKS:
                nc.gpsimd.tensor_tensor(
                    out=by_run(weighted),
                    in0=by_run(expert_outs[SHARED]),
                    in1=by_chunk(gate_sbuf[:, GPSIMD_TASKS.index(t)]),
                    op=ALU.mult,
                )
            else:
                nc.vector.tensor_tensor(
                    out=by_run(weighted),
                    in0=by_run(expert_outs[SHARED if half == COMMON else t]),
                    in1=gate_T(t, half),
                    op=ALU.mult,
                )
            for c in range(CHUNKS):
                nc.tensor.matmul(
                    out=totals[t][:, c % BLOCKS, :],
                    lhsT=weighted[:, c, :],
                    rhs=ident_f32[:],
                    is_transpose=True,
                    start=(half == COMMON and c == 0),
                    stop=(half == OWN and c == CHUNKS - 1),
                )

        def finish(t):
            nc.vector.tensor_reduce(
                out=out_sb[:, t, :],
                in_=totals[t][:].rearrange("b k (v i) -> b (k v) i", i=E_RUN),
                axis=AXIS.X,
                op=ALU.add,
            )
            nc.sync.dma_start(out=out[t], in_=out_sb[:, t, :])

        regroup_weights(SHARED)
        sort_biases()
        softmax_powers()
        transpose_activations(SHARED, 1)
        transpose_biases()
        quantise_weights(SHARED)
        softmax_sum()
        softmax_inverse()
        regroup_weights(0)
        copy_biases()
        gates_by_scalar(2)
        gates_by_scalar(3)
        quantise_activations(SHARED, 1)
        quantise_weights(0)
        gates_by_vector(0)
        gates_by_vector(1)
        transpose_activations(0, 2)
        regroup_weights(1)
        transpose_activations(2, 2)
        multiply(SHARED)
        transpose_gates()
        regroup_weights(2)
        quantise_weights(1)
        quantise_activations(0, T)
        multiply(0)
        multiply(1)
        regroup_weights(3)
        for t in range(2, T):
            quantise_weights(t)
            multiply(t)
        rectify(SHARED)
        copy_gates(2)
        copy_gates(3)
        for t in range(T):
            rectify(t)
        weigh(0, COMMON)
        weigh(1, COMMON)
        weigh(0, OWN)
        weigh(2, COMMON)
        weigh(1, OWN)
        weigh(2, OWN)
        weigh(3, COMMON)
        weigh(3, OWN)
        for t in range(T):
            finish(t)
